import numpy as np
import ml_dtypes


def mxq(x, axis, fmt="e4m3"):
    dtype, down = {"e4m3": (ml_dtypes.float8_e4m3fn, 7), "e5m2": (ml_dtypes.float8_e5m2, 14)}[fmt]
    v = np.moveaxis(np.asarray(x, np.float32).astype(ml_dtypes.bfloat16).astype(np.float64), axis, -1)
    blocks = v.reshape(v.shape[:-1] + (-1, 32))
    amax = np.abs(blocks).max(-1, keepdims=True)
    byte = np.maximum(np.where(amax > 0, np.frexp(amax)[1] - 1 + 127, 0) - down, 1)
    scale = np.exp2(byte - 127.0)
    codes = (blocks / scale).astype(np.float32).astype(dtype).astype(np.float64)
    return np.moveaxis((codes * scale).reshape(v.shape), -1, axis)


WIDE = False


def mx_kscale(k):
    if not WIDE:
        return np.ones(k)
    levels = np.array([20, -20, 10, -10, 0])
    a = np.random.permutation(np.resize(levels, k // 512 * 4)).reshape(k // 512, 4)
    idx = np.arange(k)
    return np.exp2(a[idx // 512, idx % 128 // 32])


BF16 = ml_dtypes.bfloat16


def bf(x):
    return np.asarray(x, np.float32).astype(BF16)


def f64(x):
    return np.asarray(x).astype(np.float64)


M, I0, I1, I2, N0, N1, N2 = 512, 1024, 2048, 4096, 1024, 1024, 2048
N = N0 + N1 + N2


def block(fan_in, fan_out, u):
    return bf(np.random.uniform(-1.0, 1.0, (fan_in, fan_out)) / np.sqrt(fan_in) / u[None, :])


def setup_inputs():
    u = mx_kscale(N)
    x = bf(np.random.standard_normal((M, I2)))
    w0 = block(I0, N0, u[:N0])
    w1 = block(I1, N1, u[N0:N0 + N1])
    w2 = block(I2, N2, u[N0 + N1:])
    bias = bf(np.random.standard_normal(N) * 0.1)
    g = np.random.standard_normal((M, N)) * np.exp2(np.random.randint(-12, 1, (M, 1))) * 8.0 * u
    return {"x": x, "w0": w0, "w1": w1, "w2": w2, "bias": bias, "grad_out": bf(g)}


def reference(x, w0, w1, w2, bias, grad_out):
    gq = mxq(f64(grad_out), 1, "e5m2")
    p0 = gq[:, :N0] @ mxq(f64(w0), 1, "e4m3").T
    p1 = gq[:, N0:N0 + N1] @ mxq(f64(w1), 1, "e4m3").T
    p2 = gq[:, N0 + N1:] @ mxq(f64(w2), 1, "e4m3").T
    gx = p2.copy()
    gx[:, :I1] += p1
    gx[:, :I0] += p0
    return gx

@@ -1,0 +1,186 @@
+from contextlib import ExitStack
+
+import concourse.mybir as mybir
+from concourse.masks import make_identity
+
+FLOPS = 2 * 512 * (1024 * 1024 + 2048 * 1024 + 4096 * 2048)
+BYTES = 2 * (1024 * 1024 + 2048 * 1024 + 4096 * 2048 + 512 * 4096) + 4 * 512 * 4096
+
+F32 = mybir.dt.float32
+BF16 = mybir.dt.bfloat16
+U32 = mybir.dt.uint32
+U8 = mybir.dt.uint8
+E4M3 = mybir.dt.float8_e4m3fn_x4
+E5M2 = mybir.dt.float8_e5m2_x4
+
+P = 128
+ROWS = 512
+PAIR_K = 1024
+PINNED = True
+RAW_BUFS = {2048: 3, 1024: 3}
+
+
+def tile_mlinear_kernel(tc, x, w0, w1, w2, bias, grad_out, out):
+    nc = tc.nc
+    with ExitStack() as ctx:
+        const = ctx.enter_context(tc.tile_pool(name="const", bufs=1))
+        rawp = ctx.enter_context(tc.tile_pool(name="rawp", bufs=3))
+        grp = ctx.enter_context(tc.tile_pool(name="grp", bufs=6))
+        gkeep = ctx.enter_context(tc.tile_pool(name="gkeep", bufs=1))
+        wq = ctx.enter_context(tc.tile_pool(name="wq", bufs=8))
+        outp = ctx.enter_context(tc.tile_pool(name="outp", bufs=6))
+        psum = ctx.enter_context(tc.psum_pool(name="psum", bufs=8))
+        if PINNED:
+            ctx.enter_context(tc.manual_schedule())
+
+        ident = const.tile([P, P], F32, name="ident")
+        make_identity(nc, ident[:])
+
+        def slab(label, src, klen, fmt):
+            return {"label": label, "src": src, "klen": klen, "fmt": fmt,
+                    "raw": [], "grouped": [], "codes": [], "scales": [], "done": []}
+
+        g_slab = {
+            2: slab("g2", grad_out[:, 2048:4096], 2048, E5M2),
+            1: slab("g1", grad_out[:, 1024:2048], 1024, E5M2),
+            0: slab("g0", grad_out[:, 0:1024], 1024, E5M2),
+        }
+        w_src = {2: w2, 1: w1, 0: w0}
+        w_klen = {2: 2048, 1: 1024, 0: 1024}
+        w_slab = {}
+        for c in range(8):
+            for b in (2, 1, 0):
+                if ROWS * c < w_src[b].shape[0]:
+                    w_slab[(b, c)] = slab(
+                        "w%d_%d" % (b, c), w_src[b][ROWS * c:ROWS * (c + 1), :], w_klen[b], E4M3)
+
+        def chunk_slabs(c):
+            return [(b, w_slab[(b, c)]) for b in (2, 1, 0) if (b, c) in w_slab]
+
+        order = [4, 5, 6, 7, 2, 3, 0, 1]
+        loads = [(g_slab[2], 0)]
+        loads.extend([(w_slab[(2, 4)], a) for a in range(4)])
+        loads.extend([(g_slab[2], a) for a in (1, 2, 3)])
+        for c in order[1:]:
+            for b, s in chunk_slabs(c):
+                loads.extend([(s, a) for a in range(4)])
+            if c == 7:
+                loads.extend([(g_slab[1], a) for a in range(4)])
+            if c == 3:
+                loads.extend([(g_slab[0], a) for a in range(4)])
+        live = {2048: 0, 1024: 0}
+        cursor = [0]
+
+        def prefetch():
+            while cursor[0] < len(loads):
+                s, a = loads[cursor[0]]
+                klen = s["klen"]
+                if not s["raw"]:
+                    if live[klen] >= RAW_BUFS[klen]:
+                        return
+                    live[klen] += 1
+                    s["raw"].append(rawp.tile([P, 4 * klen], BF16, name="raw_" + s["label"],
+                                              tag="raw%d" % klen, bufs=RAW_BUFS[klen]))
+                nc.sync.dma_start(out=s["raw"][0][:, a * klen:(a + 1) * klen],
+                                  in_=s["src"][P * a:P * (a + 1), :])
+                cursor[0] += 1
+
+        def quantise(s, j, first, width):
+            nc.vector.quantize_mx(
+                out=s["codes"][j][:, first:first + width].bitcast(s["fmt"]),
+                scales=s["scales"][j][:, first:first + width],
+                in_=s["grouped"][j][:, 4 * first:4 * (first + width)],
+            )
+
+        def transpose_rows(s, a):
+            prefetch()
+            klen = s["klen"]
+            pairs = klen // PAIR_K
+            is_g = s["fmt"] == E5M2
+            if not s["grouped"]:
+                for j in range(pairs):
+                    s["grouped"].append(grp.tile([P, 4 * PAIR_K], BF16, name="grp_" + s["label"],
+                                                 tag="grouped", align_bytes=64))
+                    if is_g:
+                        s["codes"].append(gkeep.tile([P, PAIR_K], U32, name="gc_%s_%d" % (s["label"], j),
+                                                     align_bytes=64))
+                        s["scales"].append(gkeep.tile([P, PAIR_K], U8, name="gs_%s_%d" % (s["label"], j),
+                                                      align_bytes=64))
+                    else:
+                        s["codes"].append(wq.tile([P, PAIR_K], U32, name="wc_" + s["label"],
+                                                  tag="wcodes", align_bytes=64))
+                        s["scales"].append(wq.tile([P, PAIR_K], U8, name="ws_" + s["label"],
+                                                   tag="wscales", align_bytes=64))
+            words = s["raw"][0][:].bitcast(F32)
+            row0 = a * (klen // 2)
+            for j in range(pairs):
+                bank = psum.tile([P, 512], F32, name="bank", tag="bank")
+                for q in range(4):
+                    first = row0 + 512 * j + P * q
+                    nc.tensor.transpose(bank[:, P * q:P * (q + 1)], words[:, first:first + P], ident[:])
+                dst = s["grouped"][j][:].bitcast(F32).rearrange("p (n c u) -> p n c u", n=2, u=2)
+                nc.scalar.copy(out=dst[:, :, P * a:P * (a + 1), :],
+                               in_=bank[:].rearrange("p (n u i) -> p n i u", n=2, u=2))
+            s["done"].append(a)
+            if is_g and s["label"] == "g2":
+                for j in range(pairs):
+                    for n in range(2):
+                        quantise(s, j, 512 * n + P * a, P)
+            elif len(s["done"]) == 4:
+                for j in range(pairs):
+                    for n in range(2):
+                        quantise(s, j, 512 * n, 512)
+            if len(s["done"]) == 4:
+                live[klen] -= 1
+
+        def transpose_slab(s):
+            for a in range(4):
+                transpose_rows(s, a)
+
+        def transpose_chunk(c):
+            for b, s in chunk_slabs(c):
+                transpose_slab(s)
+
+        def multiply_chunk(c, store_engine):
+            passes = []
+            for b, s in chunk_slabs(c):
+                for j in range(s["klen"] // PAIR_K):
+                    for n in range(2):
+                        passes.append((g_slab[b], s, j, n))
+            for m in range(4):
+                acc = psum.tile([P, 512], F32, name="acc", tag="bank")
+                for i, (g, s, j, n) in enumerate(passes):
+                    nc.tensor.matmul_mx(
+                        out=acc[:],
+                        lhsT=g["codes"][j][:, 512 * n + P * m:512 * n + P * (m + 1)].bitcast(E5M2),
+                        lhsT_scale=g["scales"][j][:, 512 * n + P * m:512 * n + P * (m + 1)],
+                        rhs=s["codes"][j][:, 512 * n:512 * (n + 1)].bitcast(E4M3),
+                        rhs_scale=s["scales"][j][:, 512 * n:512 * (n + 1)],
+                        start=(i == 0),
+                        stop=(i == len(passes) - 1),
+                    )
+                res = outp.tile([P, 512], F32, name="res", tag="res")
+                nc.vector.tensor_copy(out=res[:], in_=acc[:])
+                store_engine.dma_start(out=out[P * m:P * (m + 1), 512 * c:512 * (c + 1)], in_=res[:])
+
+        transpose_rows(g_slab[2], 0)
+        transpose_chunk(4)
+        for a in (1, 2, 3):
+            transpose_rows(g_slab[2], a)
+        multiply_chunk(4, nc.gpsimd)
+        transpose_chunk(5)
+        transpose_chunk(6)
+        multiply_chunk(5, nc.gpsimd)
+        transpose_chunk(7)
+        transpose_slab(g_slab[1])
+        multiply_chunk(6, nc.gpsimd)
+        transpose_chunk(2)
+        multiply_chunk(7, nc.gpsimd)
+        transpose_chunk(3)
+        transpose_slab(g_slab[0])
+        multiply_chunk(2, nc.gpsimd)
+        transpose_chunk(0)
+        multiply_chunk(3, nc.gpsimd)
+        transpose_chunk(1)
+        multiply_chunk(0, nc.gpsimd)
+        multiply_chunk(1, nc.sync)

@@ -17,17 +17,20 @@ P = 128
 ROWS = 512
 PAIR_K = 1024
 PINNED = True
-RAW_BUFS = {2048: 3, 1024: 3}
+RAW_BUFS = {2048: 4, 1024: 4}
+RUN_CAP = 5
+FINE = ("g2", "w2_4", "w2_5", "w2_6")
+CHUNK_ORDER = (4, 5, 6, 7, 2, 3, 0, 1)
 
 
 def tile_mlinear_kernel(tc, x, w0, w1, w2, bias, grad_out, out):
     nc = tc.nc
     with ExitStack() as ctx:
         const = ctx.enter_context(tc.tile_pool(name="const", bufs=1))
-        rawp = ctx.enter_context(tc.tile_pool(name="rawp", bufs=3))
-        grp = ctx.enter_context(tc.tile_pool(name="grp", bufs=6))
+        rawp = ctx.enter_context(tc.tile_pool(name="rawp", bufs=4))
+        grp = ctx.enter_context(tc.tile_pool(name="grp", bufs=4))
         gkeep = ctx.enter_context(tc.tile_pool(name="gkeep", bufs=1))
-        wq = ctx.enter_context(tc.tile_pool(name="wq", bufs=8))
+        wq = ctx.enter_context(tc.tile_pool(name="wq", bufs=6))
         outp = ctx.enter_context(tc.tile_pool(name="outp", bufs=6))
         psum = ctx.enter_context(tc.psum_pool(name="psum", bufs=8))
         if PINNED:
@@ -37,8 +40,8 @@ def tile_mlinear_kernel(tc, x, w0, w1, w2, bias, grad_out, out):
         make_identity(nc, ident[:])
 
         def slab(label, src, klen, fmt):
-            return {"label": label, "src": src, "klen": klen, "fmt": fmt,
-                    "raw": [], "grouped": [], "codes": [], "scales": [], "done": []}
+            return {"label": label, "src": src, "klen": klen, "fmt": fmt, "raw": [],
+                    "grouped": {}, "codes": {}, "scales": {}, "banks": {}, "left": [4 * (klen // PAIR_K)]}
 
         g_slab = {
             2: slab("g2", grad_out[:, 2048:4096], 2048, E5M2),
@@ -46,34 +49,48 @@ def tile_mlinear_kernel(tc, x, w0, w1, w2, bias, grad_out, out):
             0: slab("g0", grad_out[:, 0:1024], 1024, E5M2),
         }
         w_src = {2: w2, 1: w1, 0: w0}
-        w_klen = {2: 2048, 1: 1024, 0: 1024}
         w_slab = {}
         for c in range(8):
             for b in (2, 1, 0):
                 if ROWS * c < w_src[b].shape[0]:
-                    w_slab[(b, c)] = slab(
-                        "w%d_%d" % (b, c), w_src[b][ROWS * c:ROWS * (c + 1), :], w_klen[b], E4M3)
+                    w_slab[(b, c)] = slab("w%d_%d" % (b, c), w_src[b][ROWS * c:ROWS * (c + 1), :],
+                                          w_src[b].shape[1], E4M3)
 
-        def chunk_slabs(c):
-            return [(b, w_slab[(b, c)]) for b in (2, 1, 0) if (b, c) in w_slab]
+        blocks = []
+        pair_order = []
+        need = []
+        g_listed = []
+        for c in CHUNK_ORDER:
+            mine = [(b, j) for b in (2, 1, 0) if (b, c) in w_slab
+                    for j in range(w_slab[(b, c)]["klen"] // PAIR_K)]
+            for i, (b, j) in enumerate(mine):
+                if (b, j) not in g_listed:
+                    g_listed.append((b, j))
+                    pair_order.append((g_slab[b], j))
+                pair_order.append((w_slab[(b, c)], j))
+                need.append(len(pair_order))
+                blocks.append((c, g_slab[b], w_slab[(b, c)], j, i == 0, i == len(mine) - 1))
+        bank_order = [(s, a, j) for s, j in pair_order for a in range(4)]
 
-        order = [4, 5, 6, 7, 2, 3, 0, 1]
-        loads = [(g_slab[2], 0)]
-        loads.extend([(w_slab[(2, 4)], a) for a in range(4)])
-        loads.extend([(g_slab[2], a) for a in (1, 2, 3)])
-        for c in order[1:]:
-            for b, s in chunk_slabs(c):
-                loads.extend([(s, a) for a in range(4)])
-            if c == 7:
-                loads.extend([(g_slab[1], a) for a in range(4)])
-            if c == 3:
-                loads.extend([(g_slab[0], a) for a in range(4)])
+        upto = [0] * len(blocks)
+        upto[-1] = len(bank_order)
+        for t in range(len(blocks) - 2, -1, -1):
+            upto[t] = max(4 * need[t + 1], upto[t + 1] - RUN_CAP)
+
+        loads = []
+        seen = []
+        for s, j in pair_order:
+            if s["label"] in FINE:
+                loads.extend([(s, a, PAIR_K * j, PAIR_K) for a in range(4)])
+            elif s["label"] not in seen:
+                seen.append(s["label"])
+                loads.extend([(s, a, 0, s["klen"]) for a in range(4)])
         live = {2048: 0, 1024: 0}
         cursor = [0]
 
         def prefetch():
             while cursor[0] < len(loads):
-                s, a = loads[cursor[0]]
+                s, a, k0, kn = loads[cursor[0]]
                 klen = s["klen"]
                 if not s["raw"]:
                     if live[klen] >= RAW_BUFS[klen]:
@@ -81,106 +98,71 @@ def tile_mlinear_kernel(tc, x, w0, w1, w2, bias, grad_out, out):
                     live[klen] += 1
                     s["raw"].append(rawp.tile([P, 4 * klen], BF16, name="raw_" + s["label"],
                                               tag="raw%d" % klen, bufs=RAW_BUFS[klen]))
-                nc.sync.dma_start(out=s["raw"][0][:, a * klen:(a + 1) * klen],
-                                  in_=s["src"][P * a:P * (a + 1), :])
+                nc.sync.dma_start(out=s["raw"][0][:, a * klen + k0:a * klen + k0 + kn],
+                                  in_=s["src"][P * a:P * (a + 1), k0:k0 + kn])
                 cursor[0] += 1
 
-        def quantise(s, j, first, width):
-            nc.vector.quantize_mx(
-                out=s["codes"][j][:, first:first + width].bitcast(s["fmt"]),
-                scales=s["scales"][j][:, first:first + width],
-                in_=s["grouped"][j][:, 4 * first:4 * (first + width)],
-            )
-
-        def transpose_rows(s, a):
+        def transpose_bank(s, a, j):
             prefetch()
             klen = s["klen"]
-            pairs = klen // PAIR_K
-            is_g = s["fmt"] == E5M2
-            if not s["grouped"]:
-                for j in range(pairs):
-                    s["grouped"].append(grp.tile([P, 4 * PAIR_K], BF16, name="grp_" + s["label"],
-                                                 tag="grouped", align_bytes=64))
-                    if is_g:
-                        s["codes"].append(gkeep.tile([P, PAIR_K], U32, name="gc_%s_%d" % (s["label"], j),
-                                                     align_bytes=64))
-                        s["scales"].append(gkeep.tile([P, PAIR_K], U8, name="gs_%s_%d" % (s["label"], j),
-                                                      align_bytes=64))
-                    else:
-                        s["codes"].append(wq.tile([P, PAIR_K], U32, name="wc_" + s["label"],
-                                                  tag="wcodes", align_bytes=64))
-                        s["scales"].append(wq.tile([P, PAIR_K], U8, name="ws_" + s["label"],
-                                                   tag="wscales", align_bytes=64))
+            if j not in s["grouped"]:
+                s["banks"][j] = 0
+                s["grouped"][j] = grp.tile([P, 4 * PAIR_K], BF16, name="grp_" + s["label"],
+                                           tag="grouped", align_bytes=64)
+                if s["fmt"] == E5M2:
+                    s["codes"][j] = gkeep.tile([P, PAIR_K], U32, name="gc_%s_%d" % (s["label"], j),
+                                               align_bytes=64)
+                    s["scales"][j] = gkeep.tile([P, PAIR_K], U8, name="gs_%s_%d" % (s["label"], j),
+                                                align_bytes=64)
+                else:
+                    s["codes"][j] = wq.tile([P, PAIR_K], U32, name="wc_" + s["label"],
+                                            tag="wcodes", align_bytes=64)
+                    s["scales"][j] = wq.tile([P, PAIR_K], U8, name="ws_" + s["label"],
+                                             tag="wscales", align_bytes=64)
             words = s["raw"][0][:].bitcast(F32)
-            row0 = a * (klen // 2)
-            for j in range(pairs):
-                bank = psum.tile([P, 512], F32, name="bank", tag="bank")
-                for q in range(4):
-                    first = row0 + 512 * j + P * q
-                    nc.tensor.transpose(bank[:, P * q:P * (q + 1)], words[:, first:first + P], ident[:])
-                dst = s["grouped"][j][:].bitcast(F32).rearrange("p (n c u) -> p n c u", n=2, u=2)
-                nc.scalar.copy(out=dst[:, :, P * a:P * (a + 1), :],
-                               in_=bank[:].rearrange("p (n u i) -> p n i u", n=2, u=2))
-            s["done"].append(a)
-            if is_g and s["label"] == "g2":
-                for j in range(pairs):
-                    for n in range(2):
-                        quantise(s, j, 512 * n + P * a, P)
-            elif len(s["done"]) == 4:
-                for j in range(pairs):
-                    for n in range(2):
-                        quantise(s, j, 512 * n, 512)
-            if len(s["done"]) == 4:
+            bank = psum.tile([P, 512], F32, name="bank", tag="bank")
+            for q in range(4):
+                first = a * (klen // 2) + 512 * j + P * q
+                nc.tensor.transpose(bank[:, P * q:P * (q + 1)], words[:, first:first + P], ident[:])
+            dst = s["grouped"][j][:].bitcast(F32).rearrange("p (n c u) -> p n c u", n=2, u=2)
+            nc.scalar.copy(out=dst[:, :, P * a:P * (a + 1), :],
+                           in_=bank[:].rearrange("p (n u i) -> p n i u", n=2, u=2))
+            s["banks"][j] += 1
+            if s["banks"][j] == 4:
+                for n in range(2):
+                    nc.vector.quantize_mx(
+                        out=s["codes"][j][:, 512 * n:512 * (n + 1)].bitcast(s["fmt"]),
+                        scales=s["scales"][j][:, 512 * n:512 * (n + 1)],
+                        in_=s["grouped"][j][:, 2048 * n:2048 * (n + 1)],
+                    )
+            s["left"][0] -= 1
+            if s["left"][0] == 0:
                 live[klen] -= 1
 
-        def transpose_slab(s):
-            for a in range(4):
-                transpose_rows(s, a)
+        acc = {}
 
-        def transpose_chunk(c):
-            for b, s in chunk_slabs(c):
-                transpose_slab(s)
-
-        def multiply_chunk(c, store_engine):
-            passes = []
-            for b, s in chunk_slabs(c):
-                for j in range(s["klen"] // PAIR_K):
-                    for n in range(2):
-                        passes.append((g_slab[b], s, j, n))
+        def multiply_block(c, g, s, j, first, last, store_engine):
             for m in range(4):
-                acc = psum.tile([P, 512], F32, name="acc", tag="bank")
-                for i, (g, s, j, n) in enumerate(passes):
+                if first:
+                    acc[m] = psum.tile([P, 512], F32, name="acc", tag="bank")
+                for n in range(2):
                     nc.tensor.matmul_mx(
-                        out=acc[:],
+                        out=acc[m][:],
                         lhsT=g["codes"][j][:, 512 * n + P * m:512 * n + P * (m + 1)].bitcast(E5M2),
                         lhsT_scale=g["scales"][j][:, 512 * n + P * m:512 * n + P * (m + 1)],
                         rhs=s["codes"][j][:, 512 * n:512 * (n + 1)].bitcast(E4M3),
                         rhs_scale=s["scales"][j][:, 512 * n:512 * (n + 1)],
-                        start=(i == 0),
-                        stop=(i == len(passes) - 1),
+                        start=(first and n == 0),
+                        stop=(last and n == 1),
                     )
-                res = outp.tile([P, 512], F32, name="res", tag="res")
-                nc.vector.tensor_copy(out=res[:], in_=acc[:])
-                store_engine.dma_start(out=out[P * m:P * (m + 1), 512 * c:512 * (c + 1)], in_=res[:])
+                if last:
+                    res = outp.tile([P, 512], F32, name="res", tag="res")
+                    nc.vector.tensor_copy(out=res[:], in_=acc[m][:])
+                    store_engine.dma_start(out=out[P * m:P * (m + 1), 512 * c:512 * (c + 1)], in_=res[:])
 
-        transpose_rows(g_slab[2], 0)
-        transpose_chunk(4)
-        for a in (1, 2, 3):
-            transpose_rows(g_slab[2], a)
-        multiply_chunk(4, nc.gpsimd)
-        transpose_chunk(5)
-        transpose_chunk(6)
-        multiply_chunk(5, nc.gpsimd)
-        transpose_chunk(7)
-        transpose_slab(g_slab[1])
-        multiply_chunk(6, nc.gpsimd)
-        transpose_chunk(2)
-        multiply_chunk(7, nc.gpsimd)
-        transpose_chunk(3)
-        transpose_slab(g_slab[0])
-        multiply_chunk(2, nc.gpsimd)
-        transpose_chunk(0)
-        multiply_chunk(3, nc.gpsimd)
-        transpose_chunk(1)
-        multiply_chunk(0, nc.gpsimd)
-        multiply_chunk(1, nc.sync)
+        done = 0
+        for t, (c, g, s, j, first, last) in enumerate(blocks):
+            while done < upto[t]:
+                transpose_bank(*bank_order[done])
+                done += 1
+            multiply_block(c, g, s, j, first, last, nc.sync if c == CHUNK_ORDER[-1] else nc.gpsimd)

@@ -17,20 +17,17 @@ P = 128
 ROWS = 512
 PAIR_K = 1024
 PINNED = True
-RAW_BUFS = {2048: 4, 1024: 4}
-RUN_CAP = 5
-FINE = ("g2", "w2_4", "w2_5", "w2_6")
-CHUNK_ORDER = (4, 5, 6, 7, 2, 3, 0, 1)
+RAW_BUFS = {2048: 3, 1024: 3}
 
 
 def tile_mlinear_kernel(tc, x, w0, w1, w2, bias, grad_out, out):
     nc = tc.nc
     with ExitStack() as ctx:
         const = ctx.enter_context(tc.tile_pool(name="const", bufs=1))
-        rawp = ctx.enter_context(tc.tile_pool(name="rawp", bufs=4))
-        grp = ctx.enter_context(tc.tile_pool(name="grp", bufs=4))
+        rawp = ctx.enter_context(tc.tile_pool(name="rawp", bufs=3))
+        grp = ctx.enter_context(tc.tile_pool(name="grp", bufs=6))
         gkeep = ctx.enter_context(tc.tile_pool(name="gkeep", bufs=1))
-        wq = ctx.enter_context(tc.tile_pool(name="wq", bufs=6))
+        wq = ctx.enter_context(tc.tile_pool(name="wq", bufs=8))
         outp = ctx.enter_context(tc.tile_pool(name="outp", bufs=6))
         psum = ctx.enter_context(tc.psum_pool(name="psum", bufs=8))
         if PINNED:
@@ -40,8 +37,8 @@ def tile_mlinear_kernel(tc, x, w0, w1, w2, bias, grad_out, out):
         make_identity(nc, ident[:])
 
         def slab(label, src, klen, fmt):
-            return {"label": label, "src": src, "klen": klen, "fmt": fmt, "raw": [],
-                    "grouped": {}, "codes": {}, "scales": {}, "banks": {}, "left": [4 * (klen // PAIR_K)]}
+            return {"label": label, "src": src, "klen": klen, "fmt": fmt,
+                    "raw": [], "grouped": [], "codes": [], "scales": [], "done": []}
 
         g_slab = {
             2: slab("g2", grad_out[:, 2048:4096], 2048, E5M2),
@@ -49,48 +46,34 @@ def tile_mlinear_kernel(tc, x, w0, w1, w2, bias, grad_out, out):
             0: slab("g0", grad_out[:, 0:1024], 1024, E5M2),
         }
         w_src = {2: w2, 1: w1, 0: w0}
+        w_klen = {2: 2048, 1: 1024, 0: 1024}
         w_slab = {}
         for c in range(8):
             for b in (2, 1, 0):
                 if ROWS * c < w_src[b].shape[0]:
-                    w_slab[(b, c)] = slab("w%d_%d" % (b, c), w_src[b][ROWS * c:ROWS * (c + 1), :],
-                                          w_src[b].shape[1], E4M3)
+                    w_slab[(b, c)] = slab(
+                        "w%d_%d" % (b, c), w_src[b][ROWS * c:ROWS * (c + 1), :], w_klen[b], E4M3)
 
-        blocks = []
-        pair_order = []
-        need = []
-        g_listed = []
-        for c in CHUNK_ORDER:
-            mine = [(b, j) for b in (2, 1, 0) if (b, c) in w_slab
-                    for j in range(w_slab[(b, c)]["klen"] // PAIR_K)]
-            for i, (b, j) in enumerate(mine):
-                if (b, j) not in g_listed:
-                    g_listed.append((b, j))
-                    pair_order.append((g_slab[b], j))
-                pair_order.append((w_slab[(b, c)], j))
-                need.append(len(pair_order))
-                blocks.append((c, g_slab[b], w_slab[(b, c)], j, i == 0, i == len(mine) - 1))
-        bank_order = [(s, a, j) for s, j in pair_order for a in range(4)]
+        def chunk_slabs(c):
+            return [(b, w_slab[(b, c)]) for b in (2, 1, 0) if (b, c) in w_slab]
 
-        upto = [0] * len(blocks)
-        upto[-1] = len(bank_order)
-        for t in range(len(blocks) - 2, -1, -1):
-            upto[t] = max(4 * need[t + 1], upto[t + 1] - RUN_CAP)
-
-        loads = []
-        seen = []
-        for s, j in pair_order:
-            if s["label"] in FINE:
-                loads.extend([(s, a, PAIR_K * j, PAIR_K) for a in range(4)])
-            elif s["label"] not in seen:
-                seen.append(s["label"])
-                loads.extend([(s, a, 0, s["klen"]) for a in range(4)])
+        order = [4, 5, 6, 7, 2, 3, 0, 1]
+        loads = [(g_slab[2], 0)]
+        loads.extend([(w_slab[(2, 4)], a) for a in range(4)])
+        loads.extend([(g_slab[2], a) for a in (1, 2, 3)])
+        for c in order[1:]:
+            for b, s in chunk_slabs(c):
+                loads.extend([(s, a) for a in range(4)])
+            if c == 7:
+                loads.extend([(g_slab[1], a) for a in range(4)])
+            if c == 3:
+                loads.extend([(g_slab[0], a) for a in range(4)])
         live = {2048: 0, 1024: 0}
         cursor = [0]
 
         def prefetch():
             while cursor[0] < len(loads):
-                s, a, k0, kn = loads[cursor[0]]
+                s, a = loads[cursor[0]]
                 klen = s["klen"]
                 if not s["raw"]:
                     if live[klen] >= RAW_BUFS[klen]:
@@ -98,71 +81,112 @@ def tile_mlinear_kernel(tc, x, w0, w1, w2, bias, grad_out, out):
                     live[klen] += 1
                     s["raw"].append(rawp.tile([P, 4 * klen], BF16, name="raw_" + s["label"],
                                               tag="raw%d" % klen, bufs=RAW_BUFS[klen]))
-                nc.sync.dma_start(out=s["raw"][0][:, a * klen + k0:a * klen + k0 + kn],
-                                  in_=s["src"][P * a:P * (a + 1), k0:k0 + kn])
+                nc.sync.dma_start(out=s["raw"][0][:, a * klen:(a + 1) * klen],
+                                  in_=s["src"][P * a:P * (a + 1), :])
                 cursor[0] += 1
 
-        def transpose_bank(s, a, j):
+        turn = [0]
+
+        def quantise(s, j, first, width):
+            nc.vector.quantize_mx(
+                out=s["codes"][j][:, first:first + width].bitcast(s["fmt"]),
+                scales=s["scales"][j][:, first:first + width],
+                in_=s["grouped"][j][:, 4 * first:4 * (first + width)],
+            )
+
+        def transpose_rows(s, a):
             prefetch()
             klen = s["klen"]
-            if j not in s["grouped"]:
-                s["banks"][j] = 0
-                s["grouped"][j] = grp.tile([P, 4 * PAIR_K], BF16, name="grp_" + s["label"],
-                                           tag="grouped", align_bytes=64)
-                if s["fmt"] == E5M2:
-                    s["codes"][j] = gkeep.tile([P, PAIR_K], U32, name="gc_%s_%d" % (s["label"], j),
-                                               align_bytes=64)
-                    s["scales"][j] = gkeep.tile([P, PAIR_K], U8, name="gs_%s_%d" % (s["label"], j),
-                                                align_bytes=64)
-                else:
-                    s["codes"][j] = wq.tile([P, PAIR_K], U32, name="wc_" + s["label"],
-                                            tag="wcodes", align_bytes=64)
-                    s["scales"][j] = wq.tile([P, PAIR_K], U8, name="ws_" + s["label"],
-                                             tag="wscales", align_bytes=64)
+            pairs = klen // PAIR_K
+            is_g = s["fmt"] == E5M2
+            if not s["grouped"]:
+                for j in range(pairs):
+                    s["grouped"].append(grp.tile([P, 4 * PAIR_K], BF16, name="grp_" + s["label"],
+                                                 tag="grouped", align_bytes=64))
+                    if is_g:
+                        s["codes"].append(gkeep.tile([P, PAIR_K], U32, name="gc_%s_%d" % (s["label"], j),
+                                                     align_bytes=64))
+                        s["scales"].append(gkeep.tile([P, PAIR_K], U8, name="gs_%s_%d" % (s["label"], j),
+                                                      align_bytes=64))
+                    else:
+                        s["codes"].append(wq.tile([P, PAIR_K], U32, name="wc_" + s["label"],
+                                                  tag="wcodes", align_bytes=64))
+                        s["scales"].append(wq.tile([P, PAIR_K], U8, name="ws_" + s["label"],
+                                                   tag="wscales", align_bytes=64))
             words = s["raw"][0][:].bitcast(F32)
-            bank = psum.tile([P, 512], F32, name="bank", tag="bank")
-            for q in range(4):
-                first = a * (klen // 2) + 512 * j + P * q
-                nc.tensor.transpose(bank[:, P * q:P * (q + 1)], words[:, first:first + P], ident[:])
-            dst = s["grouped"][j][:].bitcast(F32).rearrange("p (n c u) -> p n c u", n=2, u=2)
-            nc.scalar.copy(out=dst[:, :, P * a:P * (a + 1), :],
-                           in_=bank[:].rearrange("p (n u i) -> p n i u", n=2, u=2))
-            s["banks"][j] += 1
-            if s["banks"][j] == 4:
-                for n in range(2):
-                    nc.vector.quantize_mx(
-                        out=s["codes"][j][:, 512 * n:512 * (n + 1)].bitcast(s["fmt"]),
-                        scales=s["scales"][j][:, 512 * n:512 * (n + 1)],
-                        in_=s["grouped"][j][:, 2048 * n:2048 * (n + 1)],
-                    )
-            s["left"][0] -= 1
-            if s["left"][0] == 0:
+            row0 = a * (klen // 2)
+            for j in range(pairs):
+                bank = psum.tile([P, 512], F32, name="bank", tag="bank")
+                for q in range(4):
+                    first = row0 + 512 * j + P * q
+                    nc.tensor.transpose(bank[:, P * q:P * (q + 1)], words[:, first:first + P], ident[:])
+                dst = s["grouped"][j][:].bitcast(F32).rearrange("p (n c u) -> p n c u", n=2, u=2)
+                planes = bank[:].rearrange("p (n u i) -> p n i u", n=2, u=2)
+                if turn[0] % 2 == 0:
+                    nc.scalar.copy(out=dst[:, :, P * a:P * (a + 1), :], in_=planes)
+                else:
+                    nc.vector.tensor_copy(out=dst[:, :, P * a:P * (a + 1), :], in_=planes)
+                turn[0] += 1
+            s["done"].append(a)
+            if is_g and s["label"] == "g2":
+                for j in range(pairs):
+                    for n in range(2):
+                        quantise(s, j, 512 * n + P * a, P)
+            elif len(s["done"]) == 4:
+                for j in range(pairs):
+                    for n in range(2):
+                        quantise(s, j, 512 * n, 512)
+            if len(s["done"]) == 4:
                 live[klen] -= 1
 
-        acc = {}
+        def transpose_slab(s):
+            for a in range(4):
+                transpose_rows(s, a)
 
-        def multiply_block(c, g, s, j, first, last, store_engine):
+        def transpose_chunk(c):
+            for b, s in chunk_slabs(c):
+                transpose_slab(s)
+
+        def multiply_chunk(c, store_engine):
+            passes = []
+            for b, s in chunk_slabs(c):
+                for j in range(s["klen"] // PAIR_K):
+                    for n in range(2):
+                        passes.append((g_slab[b], s, j, n))
             for m in range(4):
-                if first:
-                    acc[m] = psum.tile([P, 512], F32, name="acc", tag="bank")
-                for n in range(2):
+                acc = psum.tile([P, 512], F32, name="acc", tag="bank")
+                for i, (g, s, j, n) in enumerate(passes):
                     nc.tensor.matmul_mx(
-                        out=acc[m][:],
+                        out=acc[:],
                         lhsT=g["codes"][j][:, 512 * n + P * m:512 * n + P * (m + 1)].bitcast(E5M2),
                         lhsT_scale=g["scales"][j][:, 512 * n + P * m:512 * n + P * (m + 1)],
                         rhs=s["codes"][j][:, 512 * n:512 * (n + 1)].bitcast(E4M3),
                         rhs_scale=s["scales"][j][:, 512 * n:512 * (n + 1)],
-                        start=(first and n == 0),
-                        stop=(last and n == 1),
+                        start=(i == 0),
+                        stop=(i == len(passes) - 1),
                     )
-                if last:
-                    res = outp.tile([P, 512], F32, name="res", tag="res")
-                    nc.vector.tensor_copy(out=res[:], in_=acc[m][:])
-                    store_engine.dma_start(out=out[P * m:P * (m + 1), 512 * c:512 * (c + 1)], in_=res[:])
+                res = outp.tile([P, 512], F32, name="res", tag="res")
+                nc.scalar.copy(out=res[:], in_=acc[:])
+                store_engine.dma_start(out=out[P * m:P * (m + 1), 512 * c:512 * (c + 1)], in_=res[:])
 
-        done = 0
-        for t, (c, g, s, j, first, last) in enumerate(blocks):
-            while done < upto[t]:
-                transpose_bank(*bank_order[done])
-                done += 1
-            multiply_block(c, g, s, j, first, last, nc.sync if c == CHUNK_ORDER[-1] else nc.gpsimd)
+        transpose_rows(g_slab[2], 0)
+        transpose_chunk(4)
+        for a in (1, 2, 3):
+            transpose_rows(g_slab[2], a)
+        multiply_chunk(4, nc.gpsimd)
+        transpose_chunk(5)
+        transpose_chunk(6)
+        multiply_chunk(5, nc.gpsimd)
+        transpose_chunk(7)
+        transpose_slab(g_slab[1])
+        multiply_chunk(6, nc.gpsimd)
+        transpose_chunk(2)
+        multiply_chunk(7, nc.gpsimd)
+        transpose_chunk(3)
+        transpose_slab(g_slab[0])
+        multiply_chunk(2, nc.gpsimd)
+        transpose_chunk(0)
+        multiply_chunk(3, nc.gpsimd)
+        transpose_chunk(1)
+        multiply_chunk(0, nc.gpsimd)
+        multiply_chunk(1, nc.sync)

@@ -17,6 +17,8 @@ P = 128
 ROWS = 512
 PAIR_K = 1024
 PINNED = True
+G_PAD = 48
+G_SLOT = 256
 RAW_BUFS = {2048: 3, 1024: 3}
 
 
@@ -85,8 +87,6 @@ def tile_mlinear_kernel(tc, x, w0, w1, w2, bias, grad_out, out):
                                   in_=s["src"][P * a:P * (a + 1), :])
                 cursor[0] += 1
 
-        turn = [0]
-
         def quantise(s, j, first, width):
             nc.vector.quantize_mx(
                 out=s["codes"][j][:, first:first + width].bitcast(s["fmt"]),
@@ -104,15 +104,15 @@ def tile_mlinear_kernel(tc, x, w0, w1, w2, bias, grad_out, out):
                     s["grouped"].append(grp.tile([P, 4 * PAIR_K], BF16, name="grp_" + s["label"],
                                                  tag="grouped", align_bytes=64))
                     if is_g:
-                        s["codes"].append(gkeep.tile([P, PAIR_K], U32, name="gc_%s_%d" % (s["label"], j),
-                                                     align_bytes=64))
-                        s["scales"].append(gkeep.tile([P, PAIR_K], U8, name="gs_%s_%d" % (s["label"], j),
-                                                      align_bytes=64))
+                        s["codes"].append(gkeep.tile([P, G_PAD + PAIR_K], U32, name="gc_%s_%d" % (s["label"], j),
+                                                     align_bytes=256))
+                        s["scales"].append(gkeep.tile([P, 8 * G_SLOT], U8, name="gs_%s_%d" % (s["label"], j),
+                                                      align_bytes=256))
                     else:
                         s["codes"].append(wq.tile([P, PAIR_K], U32, name="wc_" + s["label"],
-                                                  tag="wcodes", align_bytes=64))
+                                                  tag="wcodes", align_bytes=256))
                         s["scales"].append(wq.tile([P, PAIR_K], U8, name="ws_" + s["label"],
-                                                   tag="wscales", align_bytes=64))
+                                                   tag="wscales", align_bytes=256))
             words = s["raw"][0][:].bitcast(F32)
             row0 = a * (klen // 2)
             for j in range(pairs):
@@ -121,17 +121,17 @@ def tile_mlinear_kernel(tc, x, w0, w1, w2, bias, grad_out, out):
                     first = row0 + 512 * j + P * q
                     nc.tensor.transpose(bank[:, P * q:P * (q + 1)], words[:, first:first + P], ident[:])
                 dst = s["grouped"][j][:].bitcast(F32).rearrange("p (n c u) -> p n c u", n=2, u=2)
-                planes = bank[:].rearrange("p (n u i) -> p n i u", n=2, u=2)
-                if turn[0] % 2 == 0:
-                    nc.scalar.copy(out=dst[:, :, P * a:P * (a + 1), :], in_=planes)
-                else:
-                    nc.vector.tensor_copy(out=dst[:, :, P * a:P * (a + 1), :], in_=planes)
-                turn[0] += 1
+                nc.scalar.copy(out=dst[:, :, P * a:P * (a + 1), :],
+                               in_=bank[:].rearrange("p (n u i) -> p n i u", n=2, u=2))
             s["done"].append(a)
-            if is_g and s["label"] == "g2":
+            if is_g:
                 for j in range(pairs):
                     for n in range(2):
-                        quantise(s, j, 512 * n + P * a, P)
+                        nc.vector.quantize_mx(
+                            out=s["codes"][j][:, G_PAD + 512 * n + P * a:G_PAD + 512 * n + P * (a + 1)].bitcast(E5M2),
+                            scales=s["scales"][j][:, G_SLOT * (4 * n + a):G_SLOT * (4 * n + a) + P],
+                            in_=s["grouped"][j][:, 2048 * n + 512 * a:2048 * n + 512 * (a + 1)],
+                        )
             elif len(s["done"]) == 4:
                 for j in range(pairs):
                     for n in range(2):
@@ -158,15 +158,15 @@ def tile_mlinear_kernel(tc, x, w0, w1, w2, bias, grad_out, out):
                 for i, (g, s, j, n) in enumerate(passes):
                     nc.tensor.matmul_mx(
                         out=acc[:],
-                        lhsT=g["codes"][j][:, 512 * n + P * m:512 * n + P * (m + 1)].bitcast(E5M2),
-                        lhsT_scale=g["scales"][j][:, 512 * n + P * m:512 * n + P * (m + 1)],
+                        lhsT=g["codes"][j][:, G_PAD + 512 * n + P * m:G_PAD + 512 * n + P * (m + 1)].bitcast(E5M2),
+                        lhsT_scale=g["scales"][j][:, G_SLOT * (4 * n + m):G_SLOT * (4 * n + m) + P],
                         rhs=s["codes"][j][:, 512 * n:512 * (n + 1)].bitcast(E4M3),
                         rhs_scale=s["scales"][j][:, 512 * n:512 * (n + 1)],
                         start=(i == 0),
                         stop=(i == len(passes) - 1),
                     )
                 res = outp.tile([P, 512], F32, name="res", tag="res")
-                nc.scalar.copy(out=res[:], in_=acc[:])
+                nc.vector.tensor_copy(out=res[:], in_=acc[:])
                 store_engine.dma_start(out=out[P * m:P * (m + 1), 512 * c:512 * (c + 1)], in_=res[:])
 
         transpose_rows(g_slab[2], 0)

@@ -17,7 +17,8 @@ P = 128
 ROWS = 512
 PAIR_K = 1024
 PINNED = True
-G_PAD = 48
+G_PAD = 16
+S_PAD = 64
 G_SLOT = 256
 RAW_BUFS = {2048: 3, 1024: 3}
 
@@ -90,7 +91,7 @@ def tile_mlinear_kernel(tc, x, w0, w1, w2, bias, grad_out, out):
         def quantise(s, j, first, width):
             nc.vector.quantize_mx(
                 out=s["codes"][j][:, first:first + width].bitcast(s["fmt"]),
-                scales=s["scales"][j][:, first:first + width],
+                scales=s["scales"][j][:, S_PAD + first:S_PAD + first + width],
                 in_=s["grouped"][j][:, 4 * first:4 * (first + width)],
             )
 
@@ -106,12 +107,12 @@ def tile_mlinear_kernel(tc, x, w0, w1, w2, bias, grad_out, out):
                     if is_g:
                         s["codes"].append(gkeep.tile([P, G_PAD + PAIR_K], U32, name="gc_%s_%d" % (s["label"], j),
                                                      align_bytes=256))
-                        s["scales"].append(gkeep.tile([P, 8 * G_SLOT], U8, name="gs_%s_%d" % (s["label"], j),
+                        s["scales"].append(gkeep.tile([P, S_PAD + 8 * G_SLOT], U8, name="gs_%s_%d" % (s["label"], j),
                                                       align_bytes=256))
                     else:
                         s["codes"].append(wq.tile([P, PAIR_K], U32, name="wc_" + s["label"],
                                                   tag="wcodes", align_bytes=256))
-                        s["scales"].append(wq.tile([P, PAIR_K], U8, name="ws_" + s["label"],
+                        s["scales"].append(wq.tile([P, S_PAD + PAIR_K], U8, name="ws_" + s["label"],
                                                    tag="wscales", align_bytes=256))
             words = s["raw"][0][:].bitcast(F32)
             row0 = a * (klen // 2)
@@ -129,7 +130,7 @@ def tile_mlinear_kernel(tc, x, w0, w1, w2, bias, grad_out, out):
                     for n in range(2):
                         nc.vector.quantize_mx(
                             out=s["codes"][j][:, G_PAD + 512 * n + P * a:G_PAD + 512 * n + P * (a + 1)].bitcast(E5M2),
-                            scales=s["scales"][j][:, G_SLOT * (4 * n + a):G_SLOT * (4 * n + a) + P],
+                            scales=s["scales"][j][:, S_PAD + G_SLOT * (4 * n + a):S_PAD + G_SLOT * (4 * n + a) + P],
                             in_=s["grouped"][j][:, 2048 * n + 512 * a:2048 * n + 512 * (a + 1)],
                         )
             elif len(s["done"]) == 4:
@@ -159,9 +160,9 @@ def tile_mlinear_kernel(tc, x, w0, w1, w2, bias, grad_out, out):
                     nc.tensor.matmul_mx(
                         out=acc[:],
                         lhsT=g["codes"][j][:, G_PAD + 512 * n + P * m:G_PAD + 512 * n + P * (m + 1)].bitcast(E5M2),
-                        lhsT_scale=g["scales"][j][:, G_SLOT * (4 * n + m):G_SLOT * (4 * n + m) + P],
+                        lhsT_scale=g["scales"][j][:, S_PAD + G_SLOT * (4 * n + m):S_PAD + G_SLOT * (4 * n + m) + P],
                         rhs=s["codes"][j][:, 512 * n:512 * (n + 1)].bitcast(E4M3),
-                        rhs_scale=s["scales"][j][:, 512 * n:512 * (n + 1)],
+                        rhs_scale=s["scales"][j][:, S_PAD + 512 * n:S_PAD + 512 * (n + 1)],
                         start=(i == 0),
                         stop=(i == len(passes) - 1),
                     )

@@ -17,8 +17,9 @@ P = 128
 ROWS = 512
 PAIR_K = 1024
 PINNED = True
-G_PAD = 16
-S_PAD = 64
+G_PAD = 0
+S_PAD = 0
+GS_PAD = 128
 G_SLOT = 256
 RAW_BUFS = {2048: 3, 1024: 3}
 
@@ -107,7 +108,7 @@ def tile_mlinear_kernel(tc, x, w0, w1, w2, bias, grad_out, out):
                     if is_g:
                         s["codes"].append(gkeep.tile([P, G_PAD + PAIR_K], U32, name="gc_%s_%d" % (s["label"], j),
                                                      align_bytes=256))
-                        s["scales"].append(gkeep.tile([P, S_PAD + 8 * G_SLOT], U8, name="gs_%s_%d" % (s["label"], j),
+                        s["scales"].append(gkeep.tile([P, GS_PAD + 8 * G_SLOT], U8, name="gs_%s_%d" % (s["label"], j),
                                                       align_bytes=256))
                     else:
                         s["codes"].append(wq.tile([P, PAIR_K], U32, name="wc_" + s["label"],
@@ -130,7 +131,7 @@ def tile_mlinear_kernel(tc, x, w0, w1, w2, bias, grad_out, out):
                     for n in range(2):
                         nc.vector.quantize_mx(
                             out=s["codes"][j][:, G_PAD + 512 * n + P * a:G_PAD + 512 * n + P * (a + 1)].bitcast(E5M2),
-                            scales=s["scales"][j][:, S_PAD + G_SLOT * (4 * n + a):S_PAD + G_SLOT * (4 * n + a) + P],
+                            scales=s["scales"][j][:, GS_PAD + G_SLOT * (4 * n + a):GS_PAD + G_SLOT * (4 * n + a) + P],
                             in_=s["grouped"][j][:, 2048 * n + 512 * a:2048 * n + 512 * (a + 1)],
                         )
             elif len(s["done"]) == 4:
@@ -160,7 +161,7 @@ def tile_mlinear_kernel(tc, x, w0, w1, w2, bias, grad_out, out):
                     nc.tensor.matmul_mx(
                         out=acc[:],
                         lhsT=g["codes"][j][:, G_PAD + 512 * n + P * m:G_PAD + 512 * n + P * (m + 1)].bitcast(E5M2),
-                        lhsT_scale=g["scales"][j][:, S_PAD + G_SLOT * (4 * n + m):S_PAD + G_SLOT * (4 * n + m) + P],
+                        lhsT_scale=g["scales"][j][:, GS_PAD + G_SLOT * (4 * n + m):GS_PAD + G_SLOT * (4 * n + m) + P],
                         rhs=s["codes"][j][:, 512 * n:512 * (n + 1)].bitcast(E4M3),
                         rhs_scale=s["scales"][j][:, S_PAD + 512 * n:S_PAD + 512 * (n + 1)],
                         start=(i == 0),

@@ -17,10 +17,6 @@ P = 128
 ROWS = 512
 PAIR_K = 1024
 PINNED = True
-G_PAD = 0
-S_PAD = 0
-GS_PAD = 128
-G_SLOT = 256
 RAW_BUFS = {2048: 3, 1024: 3}
 
 
@@ -28,11 +24,11 @@ def tile_mlinear_kernel(tc, x, w0, w1, w2, bias, grad_out, out):
     nc = tc.nc
     with ExitStack() as ctx:
         const = ctx.enter_context(tc.tile_pool(name="const", bufs=1))
-        rawp = ctx.enter_context(tc.tile_pool(name="rawp", bufs=3))
-        grp = ctx.enter_context(tc.tile_pool(name="grp", bufs=6))
         gkeep = ctx.enter_context(tc.tile_pool(name="gkeep", bufs=1))
         wq = ctx.enter_context(tc.tile_pool(name="wq", bufs=8))
         outp = ctx.enter_context(tc.tile_pool(name="outp", bufs=6))
+        grp = ctx.enter_context(tc.tile_pool(name="grp", bufs=6))
+        rawp = ctx.enter_context(tc.tile_pool(name="rawp", bufs=3))
         psum = ctx.enter_context(tc.psum_pool(name="psum", bufs=8))
         if PINNED:
             ctx.enter_context(tc.manual_schedule())
@@ -92,7 +88,7 @@ def tile_mlinear_kernel(tc, x, w0, w1, w2, bias, grad_out, out):
         def quantise(s, j, first, width):
             nc.vector.quantize_mx(
                 out=s["codes"][j][:, first:first + width].bitcast(s["fmt"]),
-                scales=s["scales"][j][:, S_PAD + first:S_PAD + first + width],
+                scales=s["scales"][j][:, first:first + width],
                 in_=s["grouped"][j][:, 4 * first:4 * (first + width)],
             )
 
@@ -106,15 +102,15 @@ def tile_mlinear_kernel(tc, x, w0, w1, w2, bias, grad_out, out):
                     s["grouped"].append(grp.tile([P, 4 * PAIR_K], BF16, name="grp_" + s["label"],
                                                  tag="grouped", align_bytes=64))
                     if is_g:
-                        s["codes"].append(gkeep.tile([P, G_PAD + PAIR_K], U32, name="gc_%s_%d" % (s["label"], j),
-                                                     align_bytes=256))
-                        s["scales"].append(gkeep.tile([P, GS_PAD + 8 * G_SLOT], U8, name="gs_%s_%d" % (s["label"], j),
-                                                      align_bytes=256))
+                        s["codes"].append(gkeep.tile([P, PAIR_K], U32, name="gc_%s_%d" % (s["label"], j),
+                                                     align_bytes=64))
+                        s["scales"].append(gkeep.tile([P, PAIR_K], U8, name="gs_%s_%d" % (s["label"], j),
+                                                      align_bytes=64))
                     else:
                         s["codes"].append(wq.tile([P, PAIR_K], U32, name="wc_" + s["label"],
-                                                  tag="wcodes", align_bytes=256))
-                        s["scales"].append(wq.tile([P, S_PAD + PAIR_K], U8, name="ws_" + s["label"],
-                                                   tag="wscales", align_bytes=256))
+                                                  tag="wcodes", align_bytes=64))
+                        s["scales"].append(wq.tile([P, PAIR_K], U8, name="ws_" + s["label"],
+                                                   tag="wscales", align_bytes=64))
             words = s["raw"][0][:].bitcast(F32)
             row0 = a * (klen // 2)
             for j in range(pairs):
@@ -126,14 +122,10 @@ def tile_mlinear_kernel(tc, x, w0, w1, w2, bias, grad_out, out):
                 nc.scalar.copy(out=dst[:, :, P * a:P * (a + 1), :],
                                in_=bank[:].rearrange("p (n u i) -> p n i u", n=2, u=2))
             s["done"].append(a)
-            if is_g:
+            if is_g and s["label"] == "g2":
                 for j in range(pairs):
                     for n in range(2):
-                        nc.vector.quantize_mx(
-                            out=s["codes"][j][:, G_PAD + 512 * n + P * a:G_PAD + 512 * n + P * (a + 1)].bitcast(E5M2),
-                            scales=s["scales"][j][:, GS_PAD + G_SLOT * (4 * n + a):GS_PAD + G_SLOT * (4 * n + a) + P],
-                            in_=s["grouped"][j][:, 2048 * n + 512 * a:2048 * n + 512 * (a + 1)],
-                        )
+                        quantise(s, j, 512 * n + P * a, P)
             elif len(s["done"]) == 4:
                 for j in range(pairs):
                     for n in range(2):
@@ -160,10 +152,10 @@ def tile_mlinear_kernel(tc, x, w0, w1, w2, bias, grad_out, out):
                 for i, (g, s, j, n) in enumerate(passes):
                     nc.tensor.matmul_mx(
                         out=acc[:],
-                        lhsT=g["codes"][j][:, G_PAD + 512 * n + P * m:G_PAD + 512 * n + P * (m + 1)].bitcast(E5M2),
-                        lhsT_scale=g["scales"][j][:, GS_PAD + G_SLOT * (4 * n + m):GS_PAD + G_SLOT * (4 * n + m) + P],
+                        lhsT=g["codes"][j][:, 512 * n + P * m:512 * n + P * (m + 1)].bitcast(E5M2),
+                        lhsT_scale=g["scales"][j][:, 512 * n + P * m:512 * n + P * (m + 1)],
                         rhs=s["codes"][j][:, 512 * n:512 * (n + 1)].bitcast(E4M3),
-                        rhs_scale=s["scales"][j][:, S_PAD + 512 * n:S_PAD + 512 * (n + 1)],
+                        rhs_scale=s["scales"][j][:, 512 * n:512 * (n + 1)],
                         start=(i == 0),
                         stop=(i == len(passes) - 1),
                     )

@@ -16,8 +16,11 @@ E5M2 = mybir.dt.float8_e5m2_x4
 P = 128
 ROWS = 512
 PAIR_K = 1024
-PINNED = True
 RAW_BUFS = {2048: 3, 1024: 3}
+TP_BANKS = 5
+ACC_BANKS = 3
+OUT_BUFS = 14
+LAG = 6
 
 
 def tile_mlinear_kernel(tc, x, w0, w1, w2, bias, grad_out, out):
@@ -26,12 +29,11 @@ def tile_mlinear_kernel(tc, x, w0, w1, w2, bias, grad_out, out):
         const = ctx.enter_context(tc.tile_pool(name="const", bufs=1))
         gkeep = ctx.enter_context(tc.tile_pool(name="gkeep", bufs=1))
         wq = ctx.enter_context(tc.tile_pool(name="wq", bufs=8))
-        outp = ctx.enter_context(tc.tile_pool(name="outp", bufs=6))
+        outp = ctx.enter_context(tc.tile_pool(name="outp", bufs=OUT_BUFS))
         grp = ctx.enter_context(tc.tile_pool(name="grp", bufs=6))
         rawp = ctx.enter_context(tc.tile_pool(name="rawp", bufs=3))
         psum = ctx.enter_context(tc.psum_pool(name="psum", bufs=8))
-        if PINNED:
-            ctx.enter_context(tc.manual_schedule())
+        ctx.enter_context(tc.manual_schedule())
 
         ident = const.tile([P, P], F32, name="ident")
         make_identity(nc, ident[:])
@@ -71,7 +73,18 @@ def tile_mlinear_kernel(tc, x, w0, w1, w2, bias, grad_out, out):
         live = {2048: 0, 1024: 0}
         cursor = [0]
 
+        pending = []
+
+        def flush(lag):
+            while len(pending) > lag:
+                dst, res = pending.pop(0)
+                nc.sync.dma_start(out=dst, in_=res[:])
+
         def prefetch():
+            issue_loads()
+            flush(LAG if cursor[0] < len(loads) else 0)
+
+        def issue_loads():
             while cursor[0] < len(loads):
                 s, a = loads[cursor[0]]
                 klen = s["klen"]
@@ -92,7 +105,9 @@ def tile_mlinear_kernel(tc, x, w0, w1, w2, bias, grad_out, out):
                 in_=s["grouped"][j][:, 4 * first:4 * (first + width)],
             )
 
-        def transpose_rows(s, a):
+        turn = [0]
+
+        def transpose_rows(s, a, fine=False):
             prefetch()
             klen = s["klen"]
             pairs = klen // PAIR_K
@@ -114,73 +129,78 @@ def tile_mlinear_kernel(tc, x, w0, w1, w2, bias, grad_out, out):
             words = s["raw"][0][:].bitcast(F32)
             row0 = a * (klen // 2)
             for j in range(pairs):
-                bank = psum.tile([P, 512], F32, name="bank", tag="bank")
+                bank = psum.tile([P, 512], F32, name="bank", tag="tp", bufs=TP_BANKS)
                 for q in range(4):
                     first = row0 + 512 * j + P * q
                     nc.tensor.transpose(bank[:, P * q:P * (q + 1)], words[:, first:first + P], ident[:])
                 dst = s["grouped"][j][:].bitcast(F32).rearrange("p (n c u) -> p n c u", n=2, u=2)
-                nc.scalar.copy(out=dst[:, :, P * a:P * (a + 1), :],
-                               in_=bank[:].rearrange("p (n u i) -> p n i u", n=2, u=2))
+                src = bank[:].rearrange("p (n u i) -> p n i u", n=2, u=2)
+                if turn[0] % 2 == 0:
+                    nc.scalar.copy(out=dst[:, :, P * a:P * (a + 1), :], in_=src)
+                else:
+                    nc.vector.tensor_copy(out=dst[:, :, P * a:P * (a + 1), :], in_=src)
+                turn[0] += 1
             s["done"].append(a)
-            if is_g and s["label"] == "g2":
+            if len(s["done"]) == 4:
+                live[klen] -= 1
+            if fine:
                 for j in range(pairs):
                     for n in range(2):
                         quantise(s, j, 512 * n + P * a, P)
-            elif len(s["done"]) == 4:
-                for j in range(pairs):
-                    for n in range(2):
-                        quantise(s, j, 512 * n, 512)
-            if len(s["done"]) == 4:
-                live[klen] -= 1
+
+        def quantise_slab(s):
+            for j in range(s["klen"] // PAIR_K):
+                for n in range(2):
+                    quantise(s, j, 512 * n, 512)
 
         def transpose_slab(s):
             for a in range(4):
                 transpose_rows(s, a)
 
-        def transpose_chunk(c):
-            for b, s in chunk_slabs(c):
-                transpose_slab(s)
-
-        def multiply_chunk(c, store_engine):
+        def multiply(c, m):
             passes = []
             for b, s in chunk_slabs(c):
                 for j in range(s["klen"] // PAIR_K):
                     for n in range(2):
                         passes.append((g_slab[b], s, j, n))
-            for m in range(4):
-                acc = psum.tile([P, 512], F32, name="acc", tag="bank")
-                for i, (g, s, j, n) in enumerate(passes):
-                    nc.tensor.matmul_mx(
-                        out=acc[:],
-                        lhsT=g["codes"][j][:, 512 * n + P * m:512 * n + P * (m + 1)].bitcast(E5M2),
-                        lhsT_scale=g["scales"][j][:, 512 * n + P * m:512 * n + P * (m + 1)],
-                        rhs=s["codes"][j][:, 512 * n:512 * (n + 1)].bitcast(E4M3),
-                        rhs_scale=s["scales"][j][:, 512 * n:512 * (n + 1)],
-                        start=(i == 0),
-                        stop=(i == len(passes) - 1),
-                    )
-                res = outp.tile([P, 512], F32, name="res", tag="res")
-                nc.vector.tensor_copy(out=res[:], in_=acc[:])
-                store_engine.dma_start(out=out[P * m:P * (m + 1), 512 * c:512 * (c + 1)], in_=res[:])
+            acc = psum.tile([P, 512], F32, name="acc", tag="acc", bufs=ACC_BANKS)
+            for i, (g, s, j, n) in enumerate(passes):
+                nc.tensor.matmul_mx(
+                    out=acc[:],
+                    lhsT=g["codes"][j][:, 512 * n + P * m:512 * n + P * (m + 1)].bitcast(E5M2),
+                    lhsT_scale=g["scales"][j][:, 512 * n + P * m:512 * n + P * (m + 1)],
+                    rhs=s["codes"][j][:, 512 * n:512 * (n + 1)].bitcast(E4M3),
+                    rhs_scale=s["scales"][j][:, 512 * n:512 * (n + 1)],
+                    start=(i == 0),
+                    stop=(i == len(passes) - 1),
+                )
+            res = outp.tile([P, 512], F32, name="res", tag="res")
+            nc.scalar.copy(out=res[:], in_=acc[:])
+            pending.append((out[P * m:P * (m + 1), 512 * c:512 * (c + 1)], res))
+            prefetch()
 
-        transpose_rows(g_slab[2], 0)
-        transpose_chunk(4)
-        for a in (1, 2, 3):
-            transpose_rows(g_slab[2], a)
-        multiply_chunk(4, nc.gpsimd)
-        transpose_chunk(5)
-        transpose_chunk(6)
-        multiply_chunk(5, nc.gpsimd)
-        transpose_chunk(7)
-        transpose_slab(g_slab[1])
-        multiply_chunk(6, nc.gpsimd)
-        transpose_chunk(2)
-        multiply_chunk(7, nc.gpsimd)
-        transpose_chunk(3)
-        transpose_slab(g_slab[0])
-        multiply_chunk(2, nc.gpsimd)
-        transpose_chunk(0)
-        multiply_chunk(3, nc.gpsimd)
-        transpose_chunk(1)
-        multiply_chunk(0, nc.gpsimd)
-        multiply_chunk(1, nc.sync)
+        transpose_rows(g_slab[2], 0, fine=True)
+        for a in range(4):
+            transpose_rows(w_slab[(2, 4)], a, fine=True)
+        transpose_rows(g_slab[2], 1, fine=True)
+        multiply(4, 0)
+        transpose_rows(g_slab[2], 2, fine=True)
+        multiply(4, 1)
+        transpose_rows(g_slab[2], 3, fine=True)
+        multiply(4, 2)
+        extra = {7: g_slab[1], 3: g_slab[0]}
+        for i in range(1, 8):
+            nxt, cur = order[i], order[i - 1]
+            todo = [s for b, s in chunk_slabs(nxt)]
+            if nxt in extra:
+                todo.append(extra[nxt])
+            for s in todo:
+                transpose_slab(s)
+            for s in todo:
+                quantise_slab(s)
+            for m in range(4):
+                if cur == 4 and m < 3:
+                    continue
+                multiply(cur, m)
+        for m in range(4):
+            multiply(order[7], m)

@@ -21,6 +21,7 @@ TP_BANKS = 5
 ACC_BANKS = 3
 OUT_BUFS = 14
 LAG = 6
+WHOLE_FROM = 2
 
 
 def tile_mlinear_kernel(tc, x, w0, w1, w2, bias, grad_out, out):
@@ -63,13 +64,16 @@ def tile_mlinear_kernel(tc, x, w0, w1, w2, bias, grad_out, out):
         loads = [(g_slab[2], 0)]
         loads.extend([(w_slab[(2, 4)], a) for a in range(4)])
         loads.extend([(g_slab[2], a) for a in (1, 2, 3)])
-        for c in order[1:]:
+        for i, c in enumerate(order):
+            if i == 0:
+                continue
+            parts = [None] if i >= WHOLE_FROM else [0, 1, 2, 3]
             for b, s in chunk_slabs(c):
-                loads.extend([(s, a) for a in range(4)])
+                loads.extend([(s, a) for a in parts])
             if c == 7:
-                loads.extend([(g_slab[1], a) for a in range(4)])
+                loads.extend([(g_slab[1], a) for a in parts])
             if c == 3:
-                loads.extend([(g_slab[0], a) for a in range(4)])
+                loads.extend([(g_slab[0], a) for a in parts])
         live = {2048: 0, 1024: 0}
         cursor = [0]
 
@@ -94,8 +98,12 @@ def tile_mlinear_kernel(tc, x, w0, w1, w2, bias, grad_out, out):
                     live[klen] += 1
                     s["raw"].append(rawp.tile([P, 4 * klen], BF16, name="raw_" + s["label"],
                                               tag="raw%d" % klen, bufs=RAW_BUFS[klen]))
-                nc.sync.dma_start(out=s["raw"][0][:, a * klen:(a + 1) * klen],
-                                  in_=s["src"][P * a:P * (a + 1), :])
+                if a is None:
+                    nc.sync.dma_start(out=s["raw"][0][:].rearrange("p (a k) -> p a k", a=4),
+                                      in_=s["src"].rearrange("(a p) k -> p a k", p=P))
+                else:
+                    nc.sync.dma_start(out=s["raw"][0][:, a * klen:(a + 1) * klen],
+                                      in_=s["src"][P * a:P * (a + 1), :])
                 cursor[0] += 1
 
         def quantise(s, j, first, width):

@@ -22,6 +22,7 @@ ACC_BANKS = 3
 OUT_BUFS = 14
 LAG = 6
 WHOLE_FROM = 2
+RUN_BANKS = 8
 
 
 def tile_mlinear_kernel(tc, x, w0, w1, w2, bias, grad_out, out):
@@ -202,13 +203,21 @@ def tile_mlinear_kernel(tc, x, w0, w1, w2, bias, grad_out, out):
             todo = [s for b, s in chunk_slabs(nxt)]
             if nxt in extra:
                 todo.append(extra[nxt])
+            portions = [[]]
             for s in todo:
-                transpose_slab(s)
-            for s in todo:
-                quantise_slab(s)
-            for m in range(4):
-                if cur == 4 and m < 3:
-                    continue
-                multiply(cur, m)
+                banks = 4 * (s["klen"] // PAIR_K)
+                if portions[-1] and sum(4 * (t["klen"] // PAIR_K) for t in portions[-1]) + banks > RUN_BANKS:
+                    portions.append([])
+                portions[-1].append(s)
+            groups = [m for m in range(4) if not (cur == 4 and m < 3)]
+            share = (len(groups) + len(portions) - 1) // len(portions)
+            for portion in portions:
+                for s in portion:
+                    transpose_slab(s)
+                for s in portion:
+                    quantise_slab(s)
+                for m in groups[:share]:
+                    multiply(cur, m)
+                groups = groups[share:]
         for m in range(4):
             multiply(order[7], m)

@@ -19,10 +19,15 @@ PAIR_K = 1024
 RAW_BUFS = {2048: 3, 1024: 3}
 TP_BANKS = 5
 ACC_BANKS = 3
-OUT_BUFS = 14
+OUT_BUFS = 18
 LAG = 6
-WHOLE_FROM = 2
-RUN_BANKS = 8
+WHOLE_FROM = 3
+WARM_FIRST = 8
+WARM_EACH = 1
+HEAD_GROUPS = 2
+EARLY = 0
+EARLY_BANKS = 4
+RUN_BANKS = 12
 
 
 def tile_mlinear_kernel(tc, x, w0, w1, w2, bias, grad_out, out):
@@ -39,6 +44,16 @@ def tile_mlinear_kernel(tc, x, w0, w1, w2, bias, grad_out, out):
 
         ident = const.tile([P, P], F32, name="ident")
         make_identity(nc, ident[:])
+
+        zeros = const.tile([P, 512], BF16, name="zeros")
+        nc.vector.memset(zeros[:], 0.0)
+        idle = psum.tile([P, 512], F32, name="idle", tag="acc", bufs=ACC_BANKS)
+
+        def keep_warm(count):
+            for i in range(count):
+                nc.tensor.matmul(idle[:], lhsT=zeros[:, 0:P], rhs=zeros[:], start=True, stop=True)
+
+        keep_warm(WARM_FIRST)
 
         def slab(label, src, klen, fmt):
             return {"label": label, "src": src, "klen": klen, "fmt": fmt,
@@ -144,7 +159,7 @@ def tile_mlinear_kernel(tc, x, w0, w1, w2, bias, grad_out, out):
                     nc.tensor.transpose(bank[:, P * q:P * (q + 1)], words[:, first:first + P], ident[:])
                 dst = s["grouped"][j][:].bitcast(F32).rearrange("p (n c u) -> p n c u", n=2, u=2)
                 src = bank[:].rearrange("p (n u i) -> p n i u", n=2, u=2)
-                if turn[0] % 2 == 0:
+                if fine or turn[0] % 2 == 0:
                     nc.scalar.copy(out=dst[:, :, P * a:P * (a + 1), :], in_=src)
                 else:
                     nc.vector.tensor_copy(out=dst[:, :, P * a:P * (a + 1), :], in_=src)
@@ -189,33 +204,44 @@ def tile_mlinear_kernel(tc, x, w0, w1, w2, bias, grad_out, out):
             prefetch()
 
         transpose_rows(g_slab[2], 0, fine=True)
+        keep_warm(WARM_EACH)
         for a in range(4):
             transpose_rows(w_slab[(2, 4)], a, fine=True)
+            keep_warm(WARM_EACH)
         transpose_rows(g_slab[2], 1, fine=True)
         multiply(4, 0)
         transpose_rows(g_slab[2], 2, fine=True)
         multiply(4, 1)
         transpose_rows(g_slab[2], 3, fine=True)
-        multiply(4, 2)
+        for m in range(2, HEAD_GROUPS):
+            multiply(4, m)
         extra = {7: g_slab[1], 3: g_slab[0]}
         for i in range(1, 8):
             nxt, cur = order[i], order[i - 1]
             todo = [s for b, s in chunk_slabs(nxt)]
             if nxt in extra:
                 todo.append(extra[nxt])
+            early = i <= EARLY
+            limit = EARLY_BANKS if early else RUN_BANKS
             portions = [[]]
+            filled = 0
             for s in todo:
-                banks = 4 * (s["klen"] // PAIR_K)
-                if portions[-1] and sum(4 * (t["klen"] // PAIR_K) for t in portions[-1]) + banks > RUN_BANKS:
-                    portions.append([])
-                portions[-1].append(s)
-            groups = [m for m in range(4) if not (cur == 4 and m < 3)]
+                banks = s["klen"] // PAIR_K
+                for a in range(4):
+                    if filled + banks > limit:
+                        portions.append([])
+                        filled = 0
+                    portions[-1].append((s, a))
+                    filled += banks
+            groups = [m for m in range(4) if not (cur == 4 and m < HEAD_GROUPS)]
             share = (len(groups) + len(portions) - 1) // len(portions)
             for portion in portions:
-                for s in portion:
-                    transpose_slab(s)
-                for s in portion:
-                    quantise_slab(s)
+                for s, a in portion:
+                    transpose_rows(s, a, fine=early)
+                if not early:
+                    for s, a in portion:
+                        if a == 3:
+                            quantise_slab(s)
                 for m in groups[:share]:
                     multiply(cur, m)
                 groups = groups[share:]

@@ -27,7 +27,7 @@ WARM_EACH = 1
 HEAD_GROUPS = 2
 EARLY = 0
 EARLY_BANKS = 4
-RUN_BANKS = 12
+RUN_BANKS = 8
 
 
 def tile_mlinear_kernel(tc, x, w0, w1, w2, bias, grad_out, out):

@@ -76,6 +76,14 @@ def tile_mlinear_kernel(tc, x, w0, w1, w2, bias, grad_out, out):
         def chunk_slabs(c):
             return [(b, w_slab[(b, c)]) for b in (2, 1, 0) if (b, c) in w_slab]
 
+        def to_transpose(c):
+            slabs = [s for b, s in chunk_slabs(c)]
+            if c == 2:
+                slabs = [g_slab[1], slabs[1], slabs[0]]
+            if c == 3:
+                slabs.append(g_slab[0])
+            return slabs
+
         order = [4, 5, 6, 7, 2, 3, 0, 1]
         loads = [(g_slab[2], 0)]
         loads.extend([(w_slab[(2, 4)], a) for a in range(4)])
@@ -84,12 +92,8 @@ def tile_mlinear_kernel(tc, x, w0, w1, w2, bias, grad_out, out):
             if i == 0:
                 continue
             parts = [None] if i >= WHOLE_FROM else [0, 1, 2, 3]
-            for b, s in chunk_slabs(c):
+            for s in to_transpose(c):
                 loads.extend([(s, a) for a in parts])
-            if c == 7:
-                loads.extend([(g_slab[1], a) for a in parts])
-            if c == 3:
-                loads.extend([(g_slab[0], a) for a in parts])
         live = {2048: 0, 1024: 0}
         cursor = [0]
 
@@ -211,16 +215,12 @@ def tile_mlinear_kernel(tc, x, w0, w1, w2, bias, grad_out, out):
         transpose_rows(g_slab[2], 1, fine=True)
         multiply(4, 0)
         transpose_rows(g_slab[2], 2, fine=True)
-        multiply(4, 1)
         transpose_rows(g_slab[2], 3, fine=True)
-        for m in range(2, HEAD_GROUPS):
+        for m in range(1, HEAD_GROUPS):
             multiply(4, m)
-        extra = {7: g_slab[1], 3: g_slab[0]}
         for i in range(1, 8):
             nxt, cur = order[i], order[i - 1]
-            todo = [s for b, s in chunk_slabs(nxt)]
-            if nxt in extra:
-                todo.append(extra[nxt])
+            todo = to_transpose(nxt)
             early = i <= EARLY
             limit = EARLY_BANKS if early else RUN_BANKS
             portions = [[]]

from contextlib import ExitStack

import concourse.mybir as mybir
from concourse.masks import make_identity

FLOPS = 2 * 512 * (1024 * 1024 + 2048 * 1024 + 4096 * 2048)
BYTES = 2 * (1024 * 1024 + 2048 * 1024 + 4096 * 2048 + 512 * 4096) + 4 * 512 * 4096

F32 = mybir.dt.float32
BF16 = mybir.dt.bfloat16
U32 = mybir.dt.uint32
U8 = mybir.dt.uint8
E4M3 = mybir.dt.float8_e4m3fn_x4
E5M2 = mybir.dt.float8_e5m2_x4

P = 128
ROWS = 512
PAIR_K = 1024
RAW_BUFS = {2048: 3, 1024: 3}
TP_BANKS = 5
ACC_BANKS = 3
OUT_BUFS = 18
LAG = 6
WHOLE_FROM = 3
WARM_FIRST = 8
WARM_EACH = 1
HEAD_GROUPS = 2
EARLY = 0
EARLY_BANKS = 4
RUN_BANKS = 8


def tile_mlinear_kernel(tc, x, w0, w1, w2, bias, grad_out, out):
    nc = tc.nc
    with ExitStack() as ctx:
        const = ctx.enter_context(tc.tile_pool(name="const", bufs=1))
        gkeep = ctx.enter_context(tc.tile_pool(name="gkeep", bufs=1))
        wq = ctx.enter_context(tc.tile_pool(name="wq", bufs=8))
        outp = ctx.enter_context(tc.tile_pool(name="outp", bufs=OUT_BUFS))
        grp = ctx.enter_context(tc.tile_pool(name="grp", bufs=6))
        rawp = ctx.enter_context(tc.tile_pool(name="rawp", bufs=3))
        psum = ctx.enter_context(tc.psum_pool(name="psum", bufs=8))
        ctx.enter_context(tc.manual_schedule())

        ident = const.tile([P, P], F32, name="ident")
        make_identity(nc, ident[:])

        zeros = const.tile([P, 512], BF16, name="zeros")
        nc.vector.memset(zeros[:], 0.0)
        idle = psum.tile([P, 512], F32, name="idle", tag="acc", bufs=ACC_BANKS)

        def keep_warm(count):
            for i in range(count):
                nc.tensor.matmul(idle[:], lhsT=zeros[:, 0:P], rhs=zeros[:], start=True, stop=True)

        keep_warm(WARM_FIRST)

        def slab(label, src, klen, fmt):
            return {"label": label, "src": src, "klen": klen, "fmt": fmt,
                    "raw": [], "grouped": [], "codes": [], "scales": [], "done": []}

        g_slab = {
            2: slab("g2", grad_out[:, 2048:4096], 2048, E5M2),
            1: slab("g1", grad_out[:, 1024:2048], 1024, E5M2),
            0: slab("g0", grad_out[:, 0:1024], 1024, E5M2),
        }
        w_src = {2: w2, 1: w1, 0: w0}
        w_klen = {2: 2048, 1: 1024, 0: 1024}
        w_slab = {}
        for c in range(8):
            for b in (2, 1, 0):
                if ROWS * c < w_src[b].shape[0]:
                    w_slab[(b, c)] = slab(
                        "w%d_%d" % (b, c), w_src[b][ROWS * c:ROWS * (c + 1), :], w_klen[b], E4M3)

        def chunk_slabs(c):
            return [(b, w_slab[(b, c)]) for b in (2, 1, 0) if (b, c) in w_slab]

        def to_transpose(c):
            slabs = [s for b, s in chunk_slabs(c)]
            if c == 2:
                slabs = [g_slab[1], slabs[1], slabs[0]]
            if c == 3:
                slabs.append(g_slab[0])
            return slabs

        order = [4, 5, 6, 7, 2, 3, 0, 1]
        loads = [(g_slab[2], 0)]
        loads.extend([(w_slab[(2, 4)], a) for a in range(4)])
        loads.extend([(g_slab[2], a) for a in (1, 2, 3)])
        for i, c in enumerate(order):
            if i == 0:
                continue
            parts = [None] if i >= WHOLE_FROM else [0, 1, 2, 3]
            for s in to_transpose(c):
                loads.extend([(s, a) for a in parts])
        live = {2048: 0, 1024: 0}
        cursor = [0]

        pending = []

        def flush(lag):
            while len(pending) > lag:
                dst, res = pending.pop(0)
                nc.sync.dma_start(out=dst, in_=res[:])

        def prefetch():
            issue_loads()
            flush(LAG if cursor[0] < len(loads) else 0)

        def issue_loads():
            while cursor[0] < len(loads):
                s, a = loads[cursor[0]]
                klen = s["klen"]
                if not s["raw"]:
                    if live[klen] >= RAW_BUFS[klen]:
                        return
                    live[klen] += 1
                    s["raw"].append(rawp.tile([P, 4 * klen], BF16, name="raw_" + s["label"],
                                              tag="raw%d" % klen, bufs=RAW_BUFS[klen]))
                if a is None:
                    nc.sync.dma_start(out=s["raw"][0][:].rearrange("p (a k) -> p a k", a=4),
                                      in_=s["src"].rearrange("(a p) k -> p a k", p=P))
                else:
                    nc.sync.dma_start(out=s["raw"][0][:, a * klen:(a + 1) * klen],
                                      in_=s["src"][P * a:P * (a + 1), :])
                cursor[0] += 1

        def quantise(s, j, first, width):
            nc.vector.quantize_mx(
                out=s["codes"][j][:, first:first + width].bitcast(s["fmt"]),
                scales=s["scales"][j][:, first:first + width],
                in_=s["grouped"][j][:, 4 * first:4 * (first + width)],
            )

        turn = [0]

        def transpose_rows(s, a, fine=False):
            prefetch()
            klen = s["klen"]
            pairs = klen // PAIR_K
            is_g = s["fmt"] == E5M2
            if not s["grouped"]:
                for j in range(pairs):
                    s["grouped"].append(grp.tile([P, 4 * PAIR_K], BF16, name="grp_" + s["label"],
                                                 tag="grouped", align_bytes=64))
                    if is_g:
                        s["codes"].append(gkeep.tile([P, PAIR_K], U32, name="gc_%s_%d" % (s["label"], j),
                                                     align_bytes=64))
                        s["scales"].append(gkeep.tile([P, PAIR_K], U8, name="gs_%s_%d" % (s["label"], j),
                                                      align_bytes=64))
                    else:
                        s["codes"].append(wq.tile([P, PAIR_K], U32, name="wc_" + s["label"],
                                                  tag="wcodes", align_bytes=64))
                        s["scales"].append(wq.tile([P, PAIR_K], U8, name="ws_" + s["label"],
                                                   tag="wscales", align_bytes=64))
            words = s["raw"][0][:].bitcast(F32)
            row0 = a * (klen // 2)
            for j in range(pairs):
                bank = psum.tile([P, 512], F32, name="bank", tag="tp", bufs=TP_BANKS)
                for q in range(4):
                    first = row0 + 512 * j + P * q
                    nc.tensor.transpose(bank[:, P * q:P * (q + 1)], words[:, first:first + P], ident[:])
                dst = s["grouped"][j][:].bitcast(F32).rearrange("p (n c u) -> p n c u", n=2, u=2)
                src = bank[:].rearrange("p (n u i) -> p n i u", n=2, u=2)
                if fine or turn[0] % 2 == 0:
                    nc.scalar.copy(out=dst[:, :, P * a:P * (a + 1), :], in_=src)
                else:
                    nc.vector.tensor_copy(out=dst[:, :, P * a:P * (a + 1), :], in_=src)
                turn[0] += 1
            s["done"].append(a)
            if len(s["done"]) == 4:
                live[klen] -= 1
            if fine:
                for j in range(pairs):
                    for n in range(2):
                        quantise(s, j, 512 * n + P * a, P)

        def quantise_slab(s):
            for j in range(s["klen"] // PAIR_K):
                for n in range(2):
                    quantise(s, j, 512 * n, 512)

        def transpose_slab(s):
            for a in range(4):
                transpose_rows(s, a)

        def multiply(c, m):
            passes = []
            for b, s in chunk_slabs(c):
                for j in range(s["klen"] // PAIR_K):
                    for n in range(2):
                        passes.append((g_slab[b], s, j, n))
            acc = psum.tile([P, 512], F32, name="acc", tag="acc", bufs=ACC_BANKS)
            for i, (g, s, j, n) in enumerate(passes):
                nc.tensor.matmul_mx(
                    out=acc[:],
                    lhsT=g["codes"][j][:, 512 * n + P * m:512 * n + P * (m + 1)].bitcast(E5M2),
                    lhsT_scale=g["scales"][j][:, 512 * n + P * m:512 * n + P * (m + 1)],
                    rhs=s["codes"][j][:, 512 * n:512 * (n + 1)].bitcast(E4M3),
                    rhs_scale=s["scales"][j][:, 512 * n:512 * (n + 1)],
                    start=(i == 0),
                    stop=(i == len(passes) - 1),
                )
            res = outp.tile([P, 512], F32, name="res", tag="res")
            nc.scalar.copy(out=res[:], in_=acc[:])
            pending.append((out[P * m:P * (m + 1), 512 * c:512 * (c + 1)], res))
            prefetch()

        transpose_rows(g_slab[2], 0, fine=True)
        keep_warm(WARM_EACH)
        for a in range(4):
            transpose_rows(w_slab[(2, 4)], a, fine=True)
            keep_warm(WARM_EACH)
        transpose_rows(g_slab[2], 1, fine=True)
        multiply(4, 0)
        transpose_rows(g_slab[2], 2, fine=True)
        transpose_rows(g_slab[2], 3, fine=True)
        for m in range(1, HEAD_GROUPS):
            multiply(4, m)
        for i in range(1, 8):
            nxt, cur = order[i], order[i - 1]
            todo = to_transpose(nxt)
            early = i <= EARLY
            limit = EARLY_BANKS if early else RUN_BANKS
            portions = [[]]
            filled = 0
            for s in todo:
                banks = s["klen"] // PAIR_K
                for a in range(4):
                    if filled + banks > limit:
                        portions.append([])
                        filled = 0
                    portions[-1].append((s, a))
                    filled += banks
            groups = [m for m in range(4) if not (cur == 4 and m < HEAD_GROUPS)]
            share = (len(groups) + len(portions) - 1) // len(portions)
            for portion in portions:
                for s, a in portion:
                    transpose_rows(s, a, fine=early)
                if not early:
                    for s, a in portion:
                        if a == 3:
                            quantise_slab(s)
                for m in groups[:share]:
                    multiply(cur, m)
                groups = groups[share:]
        for m in range(4):
            multiply(order[7], m)
